import numpy as np
import ml_dtypes


def mxq(x, axis, fmt="e4m3"):
    dtype, down = {"e4m3": (ml_dtypes.float8_e4m3fn, 7), "e5m2": (ml_dtypes.float8_e5m2, 14)}[fmt]
    v = np.moveaxis(np.asarray(x, np.float32).astype(ml_dtypes.bfloat16).astype(np.float64), axis, -1)
    blocks = v.reshape(v.shape[:-1] + (-1, 32))
    amax = np.abs(blocks).max(-1, keepdims=True)
    byte = np.maximum(np.where(amax > 0, np.frexp(amax)[1] - 1 + 127, 0) - down, 1)
    scale = np.exp2(byte - 127.0)
    codes = (blocks / scale).astype(np.float32).astype(dtype).astype(np.float64)
    return np.moveaxis((codes * scale).reshape(v.shape), -1, axis)


WIDE = False


def mx_kscale(k):
    if not WIDE:
        return np.ones(k)
    levels = np.array([10, -10, 5, -5, 0])
    a = np.random.permutation(np.resize(levels, k // 512 * 4)).reshape(k // 512, 4)
    idx = np.arange(k)
    return np.exp2(a[idx // 512, idx % 128 // 32])


BF16 = ml_dtypes.bfloat16


def bf(x):
    return np.asarray(x, np.float32).astype(BF16)


def f64(x):
    return np.asarray(x).astype(np.float64)


T, H, I, R = 128, 1024, 256, 512


def silu(v):
    return v / (1.0 + np.exp(-v))


def setup_inputs():
    s, t = mx_kscale(H), mx_kscale(R)
    return {
        "x": bf(np.random.standard_normal((T, H)) * s),
        "Wmean1": bf(np.random.standard_normal((I, H)) / np.sqrt(H) / s),
        "Wmean3": bf(np.random.standard_normal((I, H)) / np.sqrt(H) / s),
        "du1": bf(np.random.standard_normal((I, R)) * 0.5 / np.sqrt(R) / t),
        "dv1": bf(np.random.standard_normal((R, H)) / np.sqrt(H) / s * t[:, None]),
        "du3": bf(np.random.standard_normal((I, R)) * 0.5 / np.sqrt(R) / t),
        "dv3": bf(np.random.standard_normal((R, H)) / np.sqrt(H) / s * t[:, None]),
    }


def reference(x, Wmean1, Wmean3, du1, dv1, du3, dv3):
    xq = mxq(f64(x), 1, "e4m3")
    p3 = xq @ mxq(f64(dv3), 1, "e4m3").T
    up = (xq @ mxq(f64(Wmean3), 1, "e4m3").T) + (mxq(p3, 1, "e4m3") @ mxq(f64(du3), 1, "e4m3").T)
    p1 = xq @ mxq(f64(dv1), 1, "e4m3").T
    gate = (xq @ mxq(f64(Wmean1), 1, "e4m3").T) + (mxq(p1, 1, "e4m3") @ mxq(f64(du1), 1, "e4m3").T)
    return silu(gate) * up

@@ -1,0 +1,192 @@
+from contextlib import ExitStack
+
+import concourse.mybir as mybir
+from concourse.masks import make_identity
+
+F32 = mybir.dt.float32
+BF16 = mybir.dt.bfloat16
+U32 = mybir.dt.uint32
+U8 = mybir.dt.uint8
+FP8X4 = mybir.dt.float8_e4m3fn_x4
+SILU = mybir.ActivationFunctionType.Silu
+
+P = 128
+T, H, I, R = 128, 1024, 256, 512
+PACK = 4
+UNIT_VALUES = 1024
+UNIT_PAIRS = UNIT_VALUES // 2
+UNIT_WORDS = UNIT_VALUES // PACK
+
+FLOPS = 2 * T * (2 * H * I + 2 * H * R + 2 * R * I)
+
+
+def new_piece(pool, name, units):
+    return {
+        "units": units,
+        "raw": pool.tile([P, units * UNIT_VALUES], BF16, name=name + "_raw"),
+        "grouped": pool.tile([P, units * UNIT_VALUES], BF16, name=name + "_grouped", align_bytes=64),
+        "codes": pool.tile([P, units * UNIT_WORDS], U32, name=name + "_codes", align_bytes=64),
+        "scales": pool.tile([P, units * UNIT_WORDS], U8, name=name + "_scales", align_bytes=64),
+    }
+
+
+def flip(nc, banks, identity, piece, first_unit):
+    units = piece["units"]
+    pairs = piece["raw"][:].bitcast(F32)
+    grouped = piece["grouped"][:].bitcast(F32).rearrange(
+        "p (a c r u) -> p c a r u", a=2, c=units, u=2
+    )
+    for c in range(units):
+        bank = banks.tile([P, 4, P], F32, name="bank")
+        for j in range(4):
+            first = c * UNIT_PAIRS + j * P
+            nc.tensor.transpose(bank[:, j, :], pairs[:, first : first + P], identity[:])
+        planes = bank[:].rearrange("p (a u) r -> p a r u", u=2)
+        if (first_unit + c) % 3 == 1:
+            nc.vector.tensor_copy(out=grouped[:, c], in_=planes)
+        else:
+            nc.scalar.copy(out=grouped[:, c], in_=planes)
+
+
+def quantise(nc, piece):
+    nc.vector.quantize_mx(
+        out=piece["codes"][:].bitcast(FP8X4), scales=piece["scales"][:], in_=piece["grouped"][:]
+    )
+
+
+def mx_pass(nc, acc, stationary, moving, start, stop):
+    s_piece, s_first, s_width = stationary
+    m_piece, m_first, m_width = moving
+    s_cols = slice(s_first, s_first + s_width)
+    m_cols = slice(m_first, m_first + m_width)
+    nc.tensor.matmul_mx(
+        out=acc,
+        lhsT=s_piece["codes"][:, s_cols].bitcast(FP8X4),
+        lhsT_scale=s_piece["scales"][:, s_cols],
+        rhs=m_piece["codes"][:, m_cols].bitcast(FP8X4),
+        rhs_scale=m_piece["scales"][:, m_cols],
+        start=start,
+        stop=stop,
+    )
+
+
+def project(nc, p_bank, x_piece, dv_halves):
+    for u in range(2):
+        for e in range(2):
+            for g in range(2):
+                mx_pass(
+                    nc,
+                    p_bank[:, 2 * u + e, :],
+                    stationary=(dv_halves[u], g * 2 * P + e * P, P),
+                    moving=(x_piece, g * T, T),
+                    start=(g == 0),
+                    stop=(g == 1),
+                )
+
+
+def tile_merge_mixtralsparsemoeblock_pa_s_kernel(
+    tc, x, Wmean1, Wmean3, du1, dv1, du3, dv3, out
+):
+    nc = tc.nc
+    with ExitStack() as ctx:
+        keep = ctx.enter_context(tc.tile_pool(name="keep", bufs=1))
+        banks = ctx.enter_context(tc.psum_pool(name="banks", bufs=4))
+        sums = ctx.enter_context(tc.psum_pool(name="sums", bufs=1))
+        ctx.enter_context(tc.manual_schedule())
+
+        x_piece = new_piece(keep, "x", 1)
+        dv1_halves = [new_piece(keep, "dv1_%d" % u, 2) for u in range(2)]
+        dv3_halves = [new_piece(keep, "dv3_%d" % u, 2) for u in range(2)]
+        du1_piece = new_piece(keep, "du1", 1)
+        du3_piece = new_piece(keep, "du3", 1)
+        w1_piece = new_piece(keep, "w1", 2)
+        w3_piece = new_piece(keep, "w3", 2)
+
+        def load_rows(piece, rows, chunks):
+            nc.sync.dma_start(
+                out=piece["raw"][:].rearrange("p (c k) -> p c k", c=chunks),
+                in_=rows.rearrange("(c p) k -> p c k", c=chunks),
+            )
+
+        def load_dv(halves, dv):
+            for u in range(2):
+                nc.sync.dma_start(
+                    out=halves[u]["raw"][:],
+                    in_=dv.rearrange("(u p e) k -> u p (e k)", u=2, e=2)[u],
+                )
+
+        nc.sync.dma_start(out=x_piece["raw"][:], in_=x)
+        load_dv(dv1_halves, dv1)
+        load_dv(dv3_halves, dv3)
+        load_rows(du1_piece, du1, 2)
+        load_rows(w1_piece, Wmean1, 2)
+        load_rows(w3_piece, Wmean3, 2)
+        load_rows(du3_piece, du3, 2)
+
+        identity = keep.tile([P, P], F32, name="identity")
+        make_identity(nc, identity[:])
+        warm = keep.tile([P, 1], F32, name="warm")
+        nc.vector.memset(warm[:], 0.0)
+        nc.scalar.activation(out=warm[:], in_=warm[:], func=SILU)
+
+        p_pieces = []
+        for name in ("p1", "p3"):
+            p_pieces.append(
+                {
+                    "bank": sums.tile([P, PACK, T], F32, name=name + "_bank"),
+                    "grouped": keep.tile([P, T * PACK], BF16, name=name + "_grouped", align_bytes=64),
+                    "codes": keep.tile([P, T], U32, name=name + "_codes", align_bytes=64),
+                    "scales": keep.tile([P, T], U8, name=name + "_scales", align_bytes=64),
+                }
+            )
+        p1_piece, p3_piece = p_pieces
+        gate = sums.tile([P, I], F32, name="gate")
+        up = sums.tile([P, I], F32, name="up")
+
+        def round_p(piece):
+            nc.scalar.copy(
+                out=piece["grouped"][:].rearrange("p (t j) -> p t j", j=PACK),
+                in_=piece["bank"][:].rearrange("p j t -> p t j"),
+            )
+
+        def mean_passes(acc, w_piece):
+            for g in range(2):
+                mx_pass(nc, acc[:], (x_piece, g * T, T), (w_piece, g * I, I), start=(g == 0), stop=False)
+
+        def delta_pass(acc, p_piece, du_piece):
+            mx_pass(nc, acc[:], (p_piece, 0, T), (du_piece, 0, I), start=False, stop=True)
+
+        flip(nc, banks, identity, x_piece, 0)
+        flip(nc, banks, identity, dv1_halves[0], 1)
+        quantise(nc, x_piece)
+        flip(nc, banks, identity, dv1_halves[1], 3)
+        quantise(nc, dv1_halves[0])
+        flip(nc, banks, identity, dv3_halves[0], 5)
+        quantise(nc, dv1_halves[1])
+        flip(nc, banks, identity, dv3_halves[1], 7)
+        quantise(nc, dv3_halves[0])
+        project(nc, p1_piece["bank"], x_piece, dv1_halves)
+        flip(nc, banks, identity, du1_piece, 9)
+        quantise(nc, dv3_halves[1])
+        round_p(p1_piece)
+        flip(nc, banks, identity, w1_piece, 10)
+        quantise(nc, du1_piece)
+        quantise(nc, p1_piece)
+        project(nc, p3_piece["bank"], x_piece, dv3_halves)
+        flip(nc, banks, identity, w3_piece, 12)
+        quantise(nc, w1_piece)
+        round_p(p3_piece)
+        flip(nc, banks, identity, du3_piece, 14)
+        quantise(nc, w3_piece)
+        quantise(nc, p3_piece)
+        mean_passes(gate, w1_piece)
+        delta_pass(gate, p1_piece, du1_piece)
+        quantise(nc, du3_piece)
+        mean_passes(up, w3_piece)
+        delta_pass(up, p3_piece, du3_piece)
+
+        silu_gate = keep.tile([P, I], F32, name="silu_gate")
+        nc.scalar.activation(out=silu_gate[:], in_=gate[:], func=SILU)
+        z = keep.tile([P, I], F32, name="z")
+        nc.vector.tensor_mul(out=z[:], in0=silu_gate[:], in1=up[:])
+        nc.sync.dma_start(out=out, in_=z[:])

@@ -13,39 +13,41 @@ SILU = mybir.ActivationFunctionType.Silu
 P = 128
 T, H, I, R = 128, 1024, 256, 512
 PACK = 4
-UNIT_VALUES = 1024
-UNIT_PAIRS = UNIT_VALUES // 2
-UNIT_WORDS = UNIT_VALUES // PACK
+K_PASS = P * PACK
+BANK_PLANES = 4
 
 FLOPS = 2 * T * (2 * H * I + 2 * H * R + 2 * R * I)
 
 
-def new_piece(pool, name, units):
+def new_piece(pool, name, rows, k):
+    values = rows // P * k
     return {
-        "units": units,
-        "raw": pool.tile([P, units * UNIT_VALUES], BF16, name=name + "_raw"),
-        "grouped": pool.tile([P, units * UNIT_VALUES], BF16, name=name + "_grouped", align_bytes=64),
-        "codes": pool.tile([P, units * UNIT_WORDS], U32, name=name + "_codes", align_bytes=64),
-        "scales": pool.tile([P, units * UNIT_WORDS], U8, name=name + "_scales", align_bytes=64),
+        "chunks": rows // P,
+        "passes": k // K_PASS,
+        "raw": pool.tile([P, values], BF16, name=name + "_raw"),
+        "grouped": pool.tile([P, values], BF16, name=name + "_grouped", align_bytes=64),
+        "codes": pool.tile([P, values // PACK], U32, name=name + "_codes", align_bytes=64),
+        "scales": pool.tile([P, values // PACK], U8, name=name + "_scales", align_bytes=64),
     }
 
 
-def flip(nc, banks, identity, piece, first_unit):
-    units = piece["units"]
+def flip(nc, banks, identity, piece, copy_number):
+    chunks, passes = piece["chunks"], piece["passes"]
+    planes = 2 * passes
     pairs = piece["raw"][:].bitcast(F32)
     grouped = piece["grouped"][:].bitcast(F32).rearrange(
-        "p (a c r u) -> p c a r u", a=2, c=units, u=2
+        "p (a c r u) -> p c a r u", a=passes, c=chunks, u=2
     )
-    for c in range(units):
-        bank = banks.tile([P, 4, P], F32, name="bank")
-        for j in range(4):
-            first = c * UNIT_PAIRS + j * P
+    for c in range(chunks):
+        bank = banks.tile([P, BANK_PLANES, P], F32, name="bank")
+        for j in range(planes):
+            first = (c * planes + j) * P
             nc.tensor.transpose(bank[:, j, :], pairs[:, first : first + P], identity[:])
-        planes = bank[:].rearrange("p (a u) r -> p a r u", u=2)
-        if (first_unit + c) % 3 == 1:
-            nc.vector.tensor_copy(out=grouped[:, c], in_=planes)
+        turned = bank[:, :planes, :].rearrange("p (a u) r -> p a r u", u=2)
+        if (copy_number + c) % 3 == 2:
+            nc.vector.tensor_copy(out=grouped[:, c], in_=turned)
         else:
-            nc.scalar.copy(out=grouped[:, c], in_=planes)
+            nc.scalar.copy(out=grouped[:, c], in_=turned)
 
 
 def quantise(nc, piece):
@@ -55,33 +57,17 @@ def quantise(nc, piece):
 
 
 def mx_pass(nc, acc, stationary, moving, start, stop):
-    s_piece, s_first, s_width = stationary
-    m_piece, m_first, m_width = moving
-    s_cols = slice(s_first, s_first + s_width)
-    m_cols = slice(m_first, m_first + m_width)
+    s_piece, s_first = stationary
+    m_piece, m_first = moving
     nc.tensor.matmul_mx(
         out=acc,
-        lhsT=s_piece["codes"][:, s_cols].bitcast(FP8X4),
-        lhsT_scale=s_piece["scales"][:, s_cols],
-        rhs=m_piece["codes"][:, m_cols].bitcast(FP8X4),
-        rhs_scale=m_piece["scales"][:, m_cols],
+        lhsT=s_piece["codes"][:, s_first : s_first + P].bitcast(FP8X4),
+        lhsT_scale=s_piece["scales"][:, s_first : s_first + P],
+        rhs=m_piece["codes"][:, m_first : m_first + P].bitcast(FP8X4),
+        rhs_scale=m_piece["scales"][:, m_first : m_first + P],
         start=start,
         stop=stop,
     )
-
-
-def project(nc, p_bank, x_piece, dv_halves):
-    for u in range(2):
-        for e in range(2):
-            for g in range(2):
-                mx_pass(
-                    nc,
-                    p_bank[:, 2 * u + e, :],
-                    stationary=(dv_halves[u], g * 2 * P + e * P, P),
-                    moving=(x_piece, g * T, T),
-                    start=(g == 0),
-                    stop=(g == 1),
-                )
 
 
 def tile_merge_mixtralsparsemoeblock_pa_s_kernel(
@@ -90,38 +76,33 @@ def tile_merge_mixtralsparsemoeblock_pa_s_kernel(
     nc = tc.nc
     with ExitStack() as ctx:
         keep = ctx.enter_context(tc.tile_pool(name="keep", bufs=1))
-        banks = ctx.enter_context(tc.psum_pool(name="banks", bufs=4))
+        banks = ctx.enter_context(tc.psum_pool(name="banks", bufs=5))
         sums = ctx.enter_context(tc.psum_pool(name="sums", bufs=1))
         ctx.enter_context(tc.manual_schedule())
 
-        x_piece = new_piece(keep, "x", 1)
-        dv1_halves = [new_piece(keep, "dv1_%d" % u, 2) for u in range(2)]
-        dv3_halves = [new_piece(keep, "dv3_%d" % u, 2) for u in range(2)]
-        du1_piece = new_piece(keep, "du1", 1)
-        du3_piece = new_piece(keep, "du3", 1)
-        w1_piece = new_piece(keep, "w1", 2)
-        w3_piece = new_piece(keep, "w3", 2)
+        x_piece = new_piece(keep, "x", T, H)
+        nc.sync.dma_start(out=x_piece["raw"][:], in_=x)
 
-        def load_rows(piece, rows, chunks):
-            nc.sync.dma_start(
-                out=piece["raw"][:].rearrange("p (c k) -> p c k", c=chunks),
-                in_=rows.rearrange("(c p) k -> p c k", c=chunks),
-            )
-
-        def load_dv(halves, dv):
+        dv_halves = []
+        for name, dv in (("dv1", dv1), ("dv3", dv3)):
+            halves = [new_piece(keep, "%s_%d" % (name, u), R // 2, H) for u in range(2)]
             for u in range(2):
                 nc.sync.dma_start(
                     out=halves[u]["raw"][:],
                     in_=dv.rearrange("(u p e) k -> u p (e k)", u=2, e=2)[u],
                 )
+            dv_halves.append(halves)
 
-        nc.sync.dma_start(out=x_piece["raw"][:], in_=x)
-        load_dv(dv1_halves, dv1)
-        load_dv(dv3_halves, dv3)
-        load_rows(du1_piece, du1, 2)
-        load_rows(w1_piece, Wmean1, 2)
-        load_rows(w3_piece, Wmean3, 2)
-        load_rows(du3_piece, du3, 2)
+        blocks = []
+        for name, w, du in (("gate", Wmean1, du1), ("up", Wmean3, du3)):
+            for c in range(I // P):
+                block = {
+                    "w": new_piece(keep, "%s%d_w" % (name, c), P, H),
+                    "du": new_piece(keep, "%s%d_du" % (name, c), P, R),
+                }
+                nc.sync.dma_start(out=block["w"]["raw"][:], in_=w[c * P : (c + 1) * P, :])
+                nc.sync.dma_start(out=block["du"]["raw"][:], in_=du[c * P : (c + 1) * P, :])
+                blocks.append(block)
 
         identity = keep.tile([P, P], F32, name="identity")
         make_identity(nc, identity[:])
@@ -129,64 +110,84 @@ def tile_merge_mixtralsparsemoeblock_pa_s_kernel(
         nc.vector.memset(warm[:], 0.0)
         nc.scalar.activation(out=warm[:], in_=warm[:], func=SILU)
 
-        p_pieces = []
-        for name in ("p1", "p3"):
-            p_pieces.append(
-                {
-                    "bank": sums.tile([P, PACK, T], F32, name=name + "_bank"),
-                    "grouped": keep.tile([P, T * PACK], BF16, name=name + "_grouped", align_bytes=64),
-                    "codes": keep.tile([P, T], U32, name=name + "_codes", align_bytes=64),
-                    "scales": keep.tile([P, T], U8, name=name + "_scales", align_bytes=64),
-                }
-            )
-        p1_piece, p3_piece = p_pieces
-        gate = sums.tile([P, I], F32, name="gate")
-        up = sums.tile([P, I], F32, name="up")
+        p_pieces = [
+            {
+                "bank": sums.tile([P, PACK, T], F32, name="p%d_bank" % n, tag="side%d" % n),
+                "grouped": keep.tile([P, T * PACK], BF16, name="p%d_grouped" % n, align_bytes=64),
+                "codes": keep.tile([P, T], U32, name="p%d_codes" % n, align_bytes=64),
+                "scales": keep.tile([P, T], U8, name="p%d_scales" % n, align_bytes=64),
+            }
+            for n in range(2)
+        ]
 
-        def round_p(piece):
+        def project(n):
+            for u in range(2):
+                for e in range(2):
+                    for g in range(H // K_PASS):
+                        mx_pass(
+                            nc,
+                            p_pieces[n]["bank"][:, 2 * u + e, :],
+                            stationary=(dv_halves[n][u], g * (R // 2) + e * P),
+                            moving=(x_piece, g * T),
+                            start=(g == 0),
+                            stop=(g == H // K_PASS - 1),
+                        )
+
+        def round_p(n):
             nc.scalar.copy(
-                out=piece["grouped"][:].rearrange("p (t j) -> p t j", j=PACK),
-                in_=piece["bank"][:].rearrange("p j t -> p t j"),
+                out=p_pieces[n]["grouped"][:].rearrange("p (t j) -> p t j", j=PACK),
+                in_=p_pieces[n]["bank"][:].rearrange("p j t -> p t j"),
             )
 
-        def mean_passes(acc, w_piece):
-            for g in range(2):
-                mx_pass(nc, acc[:], (x_piece, g * T, T), (w_piece, g * I, I), start=(g == 0), stop=False)
+        def flip_block(b):
+            first_copy = 9 + 2 * b
+            flip(nc, banks, identity, blocks[b]["w"], first_copy)
+            flip(nc, banks, identity, blocks[b]["du"], first_copy + 1)
 
-        def delta_pass(acc, p_piece, du_piece):
-            mx_pass(nc, acc[:], (p_piece, 0, T), (du_piece, 0, I), start=False, stop=True)
+        def quantise_block(b):
+            quantise(nc, blocks[b]["w"])
+            quantise(nc, blocks[b]["du"])
+
+        def multiply_block(acc, b, n):
+            for g in range(H // K_PASS):
+                mx_pass(nc, acc, (x_piece, g * T), (blocks[b]["w"], g * P), start=(g == 0), stop=False)
+            mx_pass(nc, acc, (p_pieces[n], 0), (blocks[b]["du"], 0), start=False, stop=True)
 
         flip(nc, banks, identity, x_piece, 0)
-        flip(nc, banks, identity, dv1_halves[0], 1)
+        flip(nc, banks, identity, dv_halves[0][0], 1)
         quantise(nc, x_piece)
-        flip(nc, banks, identity, dv1_halves[1], 3)
-        quantise(nc, dv1_halves[0])
-        flip(nc, banks, identity, dv3_halves[0], 5)
-        quantise(nc, dv1_halves[1])
-        flip(nc, banks, identity, dv3_halves[1], 7)
-        quantise(nc, dv3_halves[0])
-        project(nc, p1_piece["bank"], x_piece, dv1_halves)
-        flip(nc, banks, identity, du1_piece, 9)
-        quantise(nc, dv3_halves[1])
-        round_p(p1_piece)
-        flip(nc, banks, identity, w1_piece, 10)
-        quantise(nc, du1_piece)
-        quantise(nc, p1_piece)
-        project(nc, p3_piece["bank"], x_piece, dv3_halves)
-        flip(nc, banks, identity, w3_piece, 12)
-        quantise(nc, w1_piece)
-        round_p(p3_piece)
-        flip(nc, banks, identity, du3_piece, 14)
-        quantise(nc, w3_piece)
-        quantise(nc, p3_piece)
-        mean_passes(gate, w1_piece)
-        delta_pass(gate, p1_piece, du1_piece)
-        quantise(nc, du3_piece)
-        mean_passes(up, w3_piece)
-        delta_pass(up, p3_piece, du3_piece)
-
+        flip(nc, banks, identity, dv_halves[0][1], 3)
+        quantise(nc, dv_halves[0][0])
+        flip(nc, banks, identity, dv_halves[1][0], 5)
+        quantise(nc, dv_halves[0][1])
+        flip(nc, banks, identity, dv_halves[1][1], 7)
+        quantise(nc, dv_halves[1][0])
+        project(0)
+        flip_block(0)
+        quantise(nc, dv_halves[1][1])
+        round_p(0)
+        flip_block(1)
+        quantise_block(0)
+        quantise(nc, p_pieces[0])
+        project(1)
+        flip_block(2)
+        quantise_block(1)
+        round_p(1)
+        gate = sums.tile([P, I], F32, name="gate")
+        multiply_block(gate[:, :P], 0, 0)
+        multiply_block(gate[:, P:], 1, 0)
+        flip_block(3)
+        quantise_block(2)
+        quantise(nc, p_pieces[1])
         silu_gate = keep.tile([P, I], F32, name="silu_gate")
         nc.scalar.activation(out=silu_gate[:], in_=gate[:], func=SILU)
+        up = [sums.tile([P, P], F32, name="up%d" % c, tag="side%d" % c) for c in range(2)]
+        multiply_block(up[0][:], 2, 1)
+        quantise_block(3)
+        multiply_block(up[1][:], 3, 1)
+
         z = keep.tile([P, I], F32, name="z")
-        nc.vector.tensor_mul(out=z[:], in0=silu_gate[:], in1=up[:])
-        nc.sync.dma_start(out=out, in_=z[:])
+        for c in range(2):
+            cols = slice(c * P, (c + 1) * P)
+            nc.vector.tensor_mul(out=z[:, cols], in0=silu_gate[:, cols], in1=up[c][:])
+            nc.sync.dma_start(out=out[:, cols], in_=z[:, cols])

@@ -15,39 +15,33 @@ T, H, I, R = 128, 1024, 256, 512
 PACK = 4
 K_PASS = P * PACK
 BANK_PLANES = 4
+LAG = 4
 
 FLOPS = 2 * T * (2 * H * I + 2 * H * R + 2 * R * I)
 
 
-def new_piece(pool, name, rows, k):
-    values = rows // P * k
+def new_piece(pool, name, k):
     return {
-        "chunks": rows // P,
         "passes": k // K_PASS,
-        "raw": pool.tile([P, values], BF16, name=name + "_raw"),
-        "grouped": pool.tile([P, values], BF16, name=name + "_grouped", align_bytes=64),
-        "codes": pool.tile([P, values // PACK], U32, name=name + "_codes", align_bytes=64),
-        "scales": pool.tile([P, values // PACK], U8, name=name + "_scales", align_bytes=64),
+        "raw": pool.tile([P, k], BF16, name=name + "_raw"),
+        "grouped": pool.tile([P, k], BF16, name=name + "_grouped", align_bytes=64),
+        "codes": pool.tile([P, k // PACK], U32, name=name + "_codes", align_bytes=64),
+        "scales": pool.tile([P, k // PACK], U8, name=name + "_scales", align_bytes=64),
     }
 
 
-def flip(nc, banks, identity, piece, copy_number):
-    chunks, passes = piece["chunks"], piece["passes"]
-    planes = 2 * passes
+def flip(nc, banks, identity, piece, number):
+    planes = 2 * piece["passes"]
     pairs = piece["raw"][:].bitcast(F32)
-    grouped = piece["grouped"][:].bitcast(F32).rearrange(
-        "p (a c r u) -> p c a r u", a=passes, c=chunks, u=2
-    )
-    for c in range(chunks):
-        bank = banks.tile([P, BANK_PLANES, P], F32, name="bank")
-        for j in range(planes):
-            first = (c * planes + j) * P
-            nc.tensor.transpose(bank[:, j, :], pairs[:, first : first + P], identity[:])
-        turned = bank[:, :planes, :].rearrange("p (a u) r -> p a r u", u=2)
-        if (copy_number + c) % 3 == 2:
-            nc.vector.tensor_copy(out=grouped[:, c], in_=turned)
-        else:
-            nc.scalar.copy(out=grouped[:, c], in_=turned)
+    bank = banks.tile([P, BANK_PLANES, P], F32, name="bank")
+    for j in range(planes):
+        nc.tensor.transpose(bank[:, j, :], pairs[:, j * P : (j + 1) * P], identity[:])
+    turned = bank[:, :planes, :].rearrange("p (a u) r -> p a r u", u=2)
+    grouped = piece["grouped"][:].bitcast(F32).rearrange("p (a r u) -> p a r u", r=P, u=2)
+    if number % 3 == 2:
+        nc.vector.tensor_copy(out=grouped, in_=turned)
+    else:
+        nc.scalar.copy(out=grouped, in_=turned)
 
 
 def quantise(nc, piece):
@@ -57,14 +51,16 @@ def quantise(nc, piece):
 
 
 def mx_pass(nc, acc, stationary, moving, start, stop):
-    s_piece, s_first = stationary
-    m_piece, m_first = moving
+    s_piece, s_pass = stationary
+    m_piece, m_pass = moving
+    s_cols = slice(s_pass * P, (s_pass + 1) * P)
+    m_cols = slice(m_pass * P, (m_pass + 1) * P)
     nc.tensor.matmul_mx(
         out=acc,
-        lhsT=s_piece["codes"][:, s_first : s_first + P].bitcast(FP8X4),
-        lhsT_scale=s_piece["scales"][:, s_first : s_first + P],
-        rhs=m_piece["codes"][:, m_first : m_first + P].bitcast(FP8X4),
-        rhs_scale=m_piece["scales"][:, m_first : m_first + P],
+        lhsT=s_piece["codes"][:, s_cols].bitcast(FP8X4),
+        lhsT_scale=s_piece["scales"][:, s_cols],
+        rhs=m_piece["codes"][:, m_cols].bitcast(FP8X4),
+        rhs_scale=m_piece["scales"][:, m_cols],
         start=start,
         stop=stop,
     )
@@ -74,35 +70,38 @@ def tile_merge_mixtralsparsemoeblock_pa_s_kernel(
     tc, x, Wmean1, Wmean3, du1, dv1, du3, dv3, out
 ):
     nc = tc.nc
+    h_passes = H // K_PASS
     with ExitStack() as ctx:
         keep = ctx.enter_context(tc.tile_pool(name="keep", bufs=1))
         banks = ctx.enter_context(tc.psum_pool(name="banks", bufs=5))
         sums = ctx.enter_context(tc.psum_pool(name="sums", bufs=1))
         ctx.enter_context(tc.manual_schedule())
 
-        x_piece = new_piece(keep, "x", T, H)
-        nc.sync.dma_start(out=x_piece["raw"][:], in_=x)
+        sequence = []
 
-        dv_halves = []
-        for name, dv in (("dv1", dv1), ("dv3", dv3)):
-            halves = [new_piece(keep, "%s_%d" % (name, u), R // 2, H) for u in range(2)]
-            for u in range(2):
-                nc.sync.dma_start(
-                    out=halves[u]["raw"][:],
-                    in_=dv.rearrange("(u p e) k -> u p (e k)", u=2, e=2)[u],
-                )
-            dv_halves.append(halves)
+        def load(name, k, rows):
+            piece = new_piece(keep, name, k)
+            nc.sync.dma_start(out=piece["raw"][:], in_=rows)
+            sequence.append(piece)
+            return piece
 
-        blocks = []
-        for name, w, du in (("gate", Wmean1, du1), ("up", Wmean3, du3)):
-            for c in range(I // P):
-                block = {
-                    "w": new_piece(keep, "%s%d_w" % (name, c), P, H),
-                    "du": new_piece(keep, "%s%d_du" % (name, c), P, R),
-                }
-                nc.sync.dma_start(out=block["w"]["raw"][:], in_=w[c * P : (c + 1) * P, :])
-                nc.sync.dma_start(out=block["du"]["raw"][:], in_=du[c * P : (c + 1) * P, :])
-                blocks.append(block)
+        x_piece = load("x", H, x)
+        dv_pieces = [
+            [
+                load("%s_%d" % (name, j), H, dv.rearrange("(u m e) k -> u e m k", u=2, e=2)[j // 2, j % 2])
+                for j in range(PACK)
+            ]
+            for name, dv in (("dv1", dv1), ("dv3", dv3))
+        ]
+        blocks = [
+            {
+                "w": load("w%d" % b, H, w[c * P : (c + 1) * P, :]),
+                "du": load("du%d" % b, R, du[c * P : (c + 1) * P, :]),
+            }
+            for b, (w, du, c) in enumerate(
+                ((Wmean1, du1, 0), (Wmean1, du1, 1), (Wmean3, du3, 0), (Wmean3, du3, 1))
+            )
+        ]
 
         identity = keep.tile([P, P], F32, name="identity")
         make_identity(nc, identity[:])
@@ -121,71 +120,44 @@ def tile_merge_mixtralsparsemoeblock_pa_s_kernel(
         ]
 
         def project(n):
-            for u in range(2):
-                for e in range(2):
-                    for g in range(H // K_PASS):
-                        mx_pass(
-                            nc,
-                            p_pieces[n]["bank"][:, 2 * u + e, :],
-                            stationary=(dv_halves[n][u], g * (R // 2) + e * P),
-                            moving=(x_piece, g * T),
-                            start=(g == 0),
-                            stop=(g == H // K_PASS - 1),
-                        )
-
-        def round_p(n):
+            for j in range(PACK):
+                for g in range(h_passes):
+                    mx_pass(
+                        nc,
+                        p_pieces[n]["bank"][:, j, :],
+                        stationary=(dv_pieces[n][j], g),
+                        moving=(x_piece, g),
+                        start=(g == 0),
+                        stop=(g == h_passes - 1),
+                    )
             nc.scalar.copy(
                 out=p_pieces[n]["grouped"][:].rearrange("p (t j) -> p t j", j=PACK),
                 in_=p_pieces[n]["bank"][:].rearrange("p j t -> p t j"),
             )
 
-        def flip_block(b):
-            first_copy = 9 + 2 * b
-            flip(nc, banks, identity, blocks[b]["w"], first_copy)
-            flip(nc, banks, identity, blocks[b]["du"], first_copy + 1)
+        copied = []
+        for number, piece in enumerate(sequence):
+            flip(nc, banks, identity, piece, number)
+            for earlier in copied:
+                quantise(nc, earlier)
+            copied = [piece]
+            for n in range(2):
+                if number == (n + 1) * PACK + LAG:
+                    project(n)
+                    copied.append(p_pieces[n])
+        for earlier in copied:
+            quantise(nc, earlier)
 
-        def quantise_block(b):
-            quantise(nc, blocks[b]["w"])
-            quantise(nc, blocks[b]["du"])
-
-        def multiply_block(acc, b, n):
-            for g in range(H // K_PASS):
-                mx_pass(nc, acc, (x_piece, g * T), (blocks[b]["w"], g * P), start=(g == 0), stop=False)
-            mx_pass(nc, acc, (p_pieces[n], 0), (blocks[b]["du"], 0), start=False, stop=True)
-
-        flip(nc, banks, identity, x_piece, 0)
-        flip(nc, banks, identity, dv_halves[0][0], 1)
-        quantise(nc, x_piece)
-        flip(nc, banks, identity, dv_halves[0][1], 3)
-        quantise(nc, dv_halves[0][0])
-        flip(nc, banks, identity, dv_halves[1][0], 5)
-        quantise(nc, dv_halves[0][1])
-        flip(nc, banks, identity, dv_halves[1][1], 7)
-        quantise(nc, dv_halves[1][0])
-        project(0)
-        flip_block(0)
-        quantise(nc, dv_halves[1][1])
-        round_p(0)
-        flip_block(1)
-        quantise_block(0)
-        quantise(nc, p_pieces[0])
-        project(1)
-        flip_block(2)
-        quantise_block(1)
-        round_p(1)
         gate = sums.tile([P, I], F32, name="gate")
-        multiply_block(gate[:, :P], 0, 0)
-        multiply_block(gate[:, P:], 1, 0)
-        flip_block(3)
-        quantise_block(2)
-        quantise(nc, p_pieces[1])
+        up = [sums.tile([P, P], F32, name="up%d" % c, tag="side%d" % c) for c in range(2)]
+        accs = [gate[:, :P], gate[:, P:], up[0][:], up[1][:]]
+        for b, block in enumerate(blocks):
+            for g in range(h_passes):
+                mx_pass(nc, accs[b], (x_piece, g), (block["w"], g), start=(g == 0), stop=False)
+            mx_pass(nc, accs[b], (p_pieces[b // 2], 0), (block["du"], 0), start=False, stop=True)
+
         silu_gate = keep.tile([P, I], F32, name="silu_gate")
         nc.scalar.activation(out=silu_gate[:], in_=gate[:], func=SILU)
-        up = [sums.tile([P, P], F32, name="up%d" % c, tag="side%d" % c) for c in range(2)]
-        multiply_block(up[0][:], 2, 1)
-        quantise_block(3)
-        multiply_block(up[1][:], 3, 1)
-
         z = keep.tile([P, I], F32, name="z")
         for c in range(2):
             cols = slice(c * P, (c + 1) * P)

@@ -23,7 +23,6 @@ FLOPS = 2 * T * (2 * H * I + 2 * H * R + 2 * R * I)
 def new_piece(pool, name, k):
     return {
         "passes": k // K_PASS,
-        "raw": pool.tile([P, k], BF16, name=name + "_raw"),
         "grouped": pool.tile([P, k], BF16, name=name + "_grouped", align_bytes=64),
         "codes": pool.tile([P, k // PACK], U32, name=name + "_codes", align_bytes=64),
         "scales": pool.tile([P, k // PACK], U8, name=name + "_scales", align_bytes=64),
@@ -32,7 +31,7 @@ def new_piece(pool, name, k):
 
 def flip(nc, banks, identity, piece, number):
     planes = 2 * piece["passes"]
-    pairs = piece["raw"][:].bitcast(F32)
+    pairs = piece["raw"].bitcast(F32)
     bank = banks.tile([P, BANK_PLANES, P], F32, name="bank")
     for j in range(planes):
         nc.tensor.transpose(bank[:, j, :], pairs[:, j * P : (j + 1) * P], identity[:])
@@ -81,18 +80,25 @@ def tile_merge_mixtralsparsemoeblock_pa_s_kernel(
 
         def load(name, k, rows):
             piece = new_piece(keep, name, k)
-            nc.sync.dma_start(out=piece["raw"][:], in_=rows)
+            raw = keep.tile([P, k], BF16, name=name + "_raw")
+            nc.sync.dma_start(out=raw[:], in_=rows)
+            piece["raw"] = raw[:]
             sequence.append(piece)
             return piece
 
         x_piece = load("x", H, x)
-        dv_pieces = [
-            [
-                load("%s_%d" % (name, j), H, dv.rearrange("(u m e) k -> u e m k", u=2, e=2)[j // 2, j % 2])
-                for j in range(PACK)
-            ]
-            for name, dv in (("dv1", dv1), ("dv3", dv3))
-        ]
+        dv_pieces = []
+        for name, dv in (("dv1", dv1), ("dv3", dv3)):
+            pieces = []
+            for u in range(2):
+                both = keep.tile([P, 2, H], BF16, name="%s_rows%d" % (name, u))
+                nc.sync.dma_start(out=both[:], in_=dv.rearrange("(u m e) k -> u m e k", u=2, e=2)[u])
+                for e in range(2):
+                    piece = new_piece(keep, "%s_%d" % (name, 2 * u + e), H)
+                    piece["raw"] = both[:, e, :]
+                    sequence.append(piece)
+                    pieces.append(piece)
+            dv_pieces.append(pieces)
         blocks = [
             {
                 "w": load("w%d" % b, H, w[c * P : (c + 1) * P, :]),

@@ -14,52 +14,59 @@ P = 128
 T, H, I, R = 128, 1024, 256, 512
 PACK = 4
 K_PASS = P * PACK
+H_PASSES = H // K_PASS
 BANK_PLANES = 4
-LAG = 4
 
 FLOPS = 2 * T * (2 * H * I + 2 * H * R + 2 * R * I)
 
 
-def new_piece(pool, name, k):
+def new_operand(pool, name, cols):
     return {
-        "passes": k // K_PASS,
-        "grouped": pool.tile([P, k], BF16, name=name + "_grouped", align_bytes=64),
-        "codes": pool.tile([P, k // PACK], U32, name=name + "_codes", align_bytes=64),
-        "scales": pool.tile([P, k // PACK], U8, name=name + "_scales", align_bytes=64),
+        "grouped": pool.tile([P, cols * PACK], BF16, name=name + "_grouped", align_bytes=64),
+        "codes": pool.tile([P, cols], U32, name=name + "_codes", align_bytes=64),
+        "scales": pool.tile([P, cols], U8, name=name + "_scales", align_bytes=64),
     }
 
 
-def flip(nc, banks, identity, piece, number):
-    planes = 2 * piece["passes"]
-    pairs = piece["raw"].bitcast(F32)
-    bank = banks.tile([P, BANK_PLANES, P], F32, name="bank")
-    for j in range(planes):
-        nc.tensor.transpose(bank[:, j, :], pairs[:, j * P : (j + 1) * P], identity[:])
-    turned = bank[:, :planes, :].rearrange("p (a u) r -> p a r u", u=2)
-    grouped = piece["grouped"][:].bitcast(F32).rearrange("p (a r u) -> p a r u", r=P, u=2)
-    if number % 3 == 2:
-        nc.vector.tensor_copy(out=grouped, in_=turned)
+def pairs(row, g):
+    return row[:, g * K_PASS : (g + 1) * K_PASS].bitcast(F32)
+
+
+def empty(nc, engine, out, in_):
+    if engine == "vector":
+        nc.vector.tensor_copy(out=out, in_=in_)
     else:
-        nc.scalar.copy(out=grouped, in_=turned)
+        nc.scalar.copy(out=out, in_=in_)
 
 
-def quantise(nc, piece):
+def turn(nc, banks, identity, sources, grouped, order, engine):
+    n = len(sources)
+    bank = banks.tile([P, BANK_PLANES, P], F32, name="bank")
+    for s, words in enumerate(sources):
+        for u in range(2):
+            nc.tensor.transpose(bank[:, 2 * s + u, :], words[:, u * P : (u + 1) * P], identity[:])
+    turned = bank[:, : 2 * n, :].rearrange("p (s u) r -> p " + order + " u", u=2)
+    empty(nc, engine, grouped.bitcast(F32).rearrange("p (" + order + " u) -> p " + order + " u", s=n, u=2), turned)
+
+
+def quantise(nc, operand, first, n):
+    cols = slice(first * P, (first + n) * P)
     nc.vector.quantize_mx(
-        out=piece["codes"][:].bitcast(FP8X4), scales=piece["scales"][:], in_=piece["grouped"][:]
+        out=operand["codes"][:, cols].bitcast(FP8X4),
+        scales=operand["scales"][:, cols],
+        in_=operand["grouped"][:, first * P * PACK : (first + n) * P * PACK],
     )
 
 
-def mx_pass(nc, acc, stationary, moving, start, stop):
-    s_piece, s_pass = stationary
-    m_piece, m_pass = moving
-    s_cols = slice(s_pass * P, (s_pass + 1) * P)
-    m_cols = slice(m_pass * P, (m_pass + 1) * P)
+def mx_pass(nc, acc, stationary, s_first, moving, m_first, m_n, start, stop):
+    s_cols = slice(s_first * P, (s_first + 1) * P)
+    m_cols = slice(m_first * P, (m_first + m_n) * P)
     nc.tensor.matmul_mx(
         out=acc,
-        lhsT=s_piece["codes"][:, s_cols].bitcast(FP8X4),
-        lhsT_scale=s_piece["scales"][:, s_cols],
-        rhs=m_piece["codes"][:, m_cols].bitcast(FP8X4),
-        rhs_scale=m_piece["scales"][:, m_cols],
+        lhsT=stationary["codes"][:, s_cols].bitcast(FP8X4),
+        lhsT_scale=stationary["scales"][:, s_cols],
+        rhs=moving["codes"][:, m_cols].bitcast(FP8X4),
+        rhs_scale=moving["scales"][:, m_cols],
         start=start,
         stop=stop,
     )
@@ -69,45 +76,26 @@ def tile_merge_mixtralsparsemoeblock_pa_s_kernel(
     tc, x, Wmean1, Wmean3, du1, dv1, du3, dv3, out
 ):
     nc = tc.nc
-    h_passes = H // K_PASS
     with ExitStack() as ctx:
         keep = ctx.enter_context(tc.tile_pool(name="keep", bufs=1))
         banks = ctx.enter_context(tc.psum_pool(name="banks", bufs=5))
         sums = ctx.enter_context(tc.psum_pool(name="sums", bufs=1))
         ctx.enter_context(tc.manual_schedule())
 
-        sequence = []
-
-        def load(name, k, rows):
-            piece = new_piece(keep, name, k)
-            raw = keep.tile([P, k], BF16, name=name + "_raw")
+        def load(name, shape, rows):
+            raw = keep.tile(shape, BF16, name=name)
             nc.sync.dma_start(out=raw[:], in_=rows)
-            piece["raw"] = raw[:]
-            sequence.append(piece)
-            return piece
+            return raw
 
-        x_piece = load("x", H, x)
-        dv_pieces = []
-        for name, dv in (("dv1", dv1), ("dv3", dv3)):
-            pieces = []
-            for u in range(2):
-                both = keep.tile([P, 2, H], BF16, name="%s_rows%d" % (name, u))
-                nc.sync.dma_start(out=both[:], in_=dv.rearrange("(u m e) k -> u m e k", u=2, e=2)[u])
-                for e in range(2):
-                    piece = new_piece(keep, "%s_%d" % (name, 2 * u + e), H)
-                    piece["raw"] = both[:, e, :]
-                    sequence.append(piece)
-                    pieces.append(piece)
-            dv_pieces.append(pieces)
-        blocks = [
-            {
-                "w": load("w%d" % b, H, w[c * P : (c + 1) * P, :]),
-                "du": load("du%d" % b, R, du[c * P : (c + 1) * P, :]),
-            }
-            for b, (w, du, c) in enumerate(
-                ((Wmean1, du1, 0), (Wmean1, du1, 1), (Wmean3, du3, 0), (Wmean3, du3, 1))
-            )
+        x_raw = load("x_raw", [P, H], x)
+        dv_raw = [
+            [load("dv%d_raw%d" % (n, u), [P, 2, H], dv.rearrange("(u m e) k -> u m e k", u=2, e=2)[u]) for u in range(2)]
+            for n, dv in enumerate((dv1, dv3))
         ]
+        w1_raw = load("w1_raw", [P, 2, H], Wmean1.rearrange("(m e) k -> m e k", e=2))
+        du1_raw = load("du1_raw", [P, 2, R], du1.rearrange("(m e) k -> m e k", e=2))
+        w3_raw = load("w3_raw", [P, 2, H], Wmean3.rearrange("(m e) k -> m e k", e=2))
+        du3_raw = [load("du3_raw%d" % c, [P, R], du3[c * P : (c + 1) * P, :]) for c in range(2)]
 
         identity = keep.tile([P, P], F32, name="identity")
         make_identity(nc, identity[:])
@@ -115,57 +103,79 @@ def tile_merge_mixtralsparsemoeblock_pa_s_kernel(
         nc.vector.memset(warm[:], 0.0)
         nc.scalar.activation(out=warm[:], in_=warm[:], func=SILU)
 
-        p_pieces = [
-            {
-                "bank": sums.tile([P, PACK, T], F32, name="p%d_bank" % n, tag="side%d" % n),
-                "grouped": keep.tile([P, T * PACK], BF16, name="p%d_grouped" % n, align_bytes=64),
-                "codes": keep.tile([P, T], U32, name="p%d_codes" % n, align_bytes=64),
-                "scales": keep.tile([P, T], U8, name="p%d_scales" % n, align_bytes=64),
-            }
-            for n in range(2)
-        ]
-
-        def project(n):
-            for j in range(PACK):
-                for g in range(h_passes):
-                    mx_pass(
-                        nc,
-                        p_pieces[n]["bank"][:, j, :],
-                        stationary=(dv_pieces[n][j], g),
-                        moving=(x_piece, g),
-                        start=(g == 0),
-                        stop=(g == h_passes - 1),
-                    )
-            nc.scalar.copy(
-                out=p_pieces[n]["grouped"][:].rearrange("p (t j) -> p t j", j=PACK),
-                in_=p_pieces[n]["bank"][:].rearrange("p j t -> p t j"),
-            )
+        x_op = new_operand(keep, "x", H_PASSES * P)
+        dv_op = [[new_operand(keep, "dv%d_%d" % (n, j), H_PASSES * P) for j in range(PACK)] for n in range(2)]
+        w_op = [[new_operand(keep, "w%d_%d" % (n, g), I) for g in range(H_PASSES)] for n in range(2)]
+        du_op = [new_operand(keep, "du%d" % n, I) for n in range(2)]
+        p_op = [new_operand(keep, "p%d" % n, T) for n in range(2)]
+        p_bank = [sums.tile([P, PACK, T], F32, name="p%d_bank" % n, tag="side%d" % n) for n in range(2)]
 
         copied = []
-        for number, piece in enumerate(sequence):
-            flip(nc, banks, identity, piece, number)
-            for earlier in copied:
-                quantise(nc, earlier)
-            copied = [piece]
-            for n in range(2):
-                if number == (n + 1) * PACK + LAG:
-                    project(n)
-                    copied.append(p_pieces[n])
-        for earlier in copied:
-            quantise(nc, earlier)
+
+        def step(todo):
+            for args in copied:
+                quantise(nc, *args)
+            copied.clear()
+            copied.extend(todo)
+
+        def turn_rows(operand, row, engine):
+            turn(nc, banks, identity, [pairs(row, g) for g in range(H_PASSES)], operand["grouped"][:], "s r", engine)
+            step([(operand, 0, H_PASSES)])
+
+        def turn_pass(operand, raw, g, engine):
+            turn(nc, banks, identity, [pairs(raw[:, e, :], g) for e in range(2)], operand["grouped"][:], "r s", engine)
+            step([(operand, 0, 2)])
+
+        def turn_half(operand, raw, c, engine):
+            cols = slice(c * P * PACK, (c + 1) * P * PACK)
+            turn(nc, banks, identity, [pairs(raw, 0)], operand["grouped"][:, cols], "s r", engine)
+            step([(operand, c, 1)])
+
+        def project(n, engine):
+            for j in range(PACK):
+                for g in range(H_PASSES):
+                    mx_pass(nc, p_bank[n][:, j, :], dv_op[n][j], g, x_op, g, 1, start=(g == 0), stop=(g == H_PASSES - 1))
+            empty(
+                nc,
+                engine,
+                p_op[n]["grouped"][:].rearrange("p (t j) -> p t j", j=PACK),
+                p_bank[n][:].rearrange("p j t -> p t j"),
+            )
+            copied.append((p_op[n], 0, 1))
+
+        turn_rows(x_op, x_raw[:], "scalar")
+        turn_rows(dv_op[0][0], dv_raw[0][0][:, 0, :], "scalar")
+        turn_rows(dv_op[0][1], dv_raw[0][0][:, 1, :], "vector")
+        turn_rows(dv_op[0][2], dv_raw[0][1][:, 0, :], "scalar")
+        turn_rows(dv_op[0][3], dv_raw[0][1][:, 1, :], "scalar")
+        turn_rows(dv_op[1][0], dv_raw[1][0][:, 0, :], "scalar")
+        turn_rows(dv_op[1][1], dv_raw[1][0][:, 1, :], "vector")
+        project(0, "scalar")
+        turn_rows(dv_op[1][2], dv_raw[1][1][:, 0, :], "scalar")
+        turn_rows(dv_op[1][3], dv_raw[1][1][:, 1, :], "vector")
+        turn_pass(w_op[0][0], w1_raw, 0, "scalar")
+        turn_pass(w_op[0][1], w1_raw, 1, "scalar")
+        turn_pass(du_op[0], du1_raw, 0, "scalar")
+        project(1, "vector")
+        turn_pass(w_op[1][0], w3_raw, 0, "scalar")
+        turn_pass(w_op[1][1], w3_raw, 1, "scalar")
+        turn_half(du_op[1], du3_raw[0][:], 0, "vector")
+        turn_half(du_op[1], du3_raw[1][:], 1, "scalar")
 
         gate = sums.tile([P, I], F32, name="gate")
-        up = [sums.tile([P, P], F32, name="up%d" % c, tag="side%d" % c) for c in range(2)]
-        accs = [gate[:, :P], gate[:, P:], up[0][:], up[1][:]]
-        for b, block in enumerate(blocks):
-            for g in range(h_passes):
-                mx_pass(nc, accs[b], (x_piece, g), (block["w"], g), start=(g == 0), stop=False)
-            mx_pass(nc, accs[b], (p_pieces[b // 2], 0), (block["du"], 0), start=False, stop=True)
-
+        for g in range(H_PASSES):
+            mx_pass(nc, gate[:], x_op, g, w_op[0][g], 0, 2, start=(g == 0), stop=False)
+        mx_pass(nc, gate[:], p_op[0], 0, du_op[0], 0, 2, start=False, stop=True)
         silu_gate = keep.tile([P, I], F32, name="silu_gate")
         nc.scalar.activation(out=silu_gate[:], in_=gate[:], func=SILU)
+        step([])
+        up = [sums.tile([P, P], F32, name="up%d" % c, tag="side%d" % c) for c in range(2)]
+        for c in range(2):
+            for g in range(H_PASSES):
+                mx_pass(nc, up[c][:], x_op, g, w_op[1][g], c, 1, start=(g == 0), stop=False)
         z = keep.tile([P, I], F32, name="z")
         for c in range(2):
             cols = slice(c * P, (c + 1) * P)
+            mx_pass(nc, up[c][:], p_op[1], 0, du_op[1], c, 1, start=False, stop=True)
             nc.vector.tensor_mul(out=z[:, cols], in0=silu_gate[:, cols], in1=up[c][:])
             nc.sync.dma_start(out=out[:, cols], in_=z[:, cols])

@@ -5,6 +5,7 @@ from concourse.masks import make_identity
 
 F32 = mybir.dt.float32
 BF16 = mybir.dt.bfloat16
+I32 = mybir.dt.int32
 U32 = mybir.dt.uint32
 U8 = mybir.dt.uint8
 FP8X4 = mybir.dt.float8_e4m3fn_x4
@@ -16,6 +17,7 @@ PACK = 4
 K_PASS = P * PACK
 H_PASSES = H // K_PASS
 BANK_PLANES = 4
+WARM_PASSES = 10
 
 FLOPS = 2 * T * (2 * H * I + 2 * H * R + 2 * R * I)
 
@@ -102,6 +104,12 @@ def tile_merge_mixtralsparsemoeblock_pa_s_kernel(
         warm = keep.tile([P, 1], F32, name="warm")
         nc.vector.memset(warm[:], 0.0)
         nc.scalar.activation(out=warm[:], in_=warm[:], func=SILU)
+        zeros = new_operand(keep, "zeros", P)
+        nc.vector.memset(zeros["grouped"][:].bitcast(I32), 0)
+        quantise(nc, zeros, 0, 1)
+        idle = banks.tile([P, BANK_PLANES, P], F32, name="bank")
+        for i in range(WARM_PASSES):
+            mx_pass(nc, idle[:, 0, :], zeros, 0, zeros, 0, 1, start=True, stop=True)
 
         x_op = new_operand(keep, "x", H_PASSES * P)
         dv_op = [[new_operand(keep, "dv%d_%d" % (n, j), H_PASSES * P) for j in range(PACK)] for n in range(2)]
@@ -150,16 +158,16 @@ def tile_merge_mixtralsparsemoeblock_pa_s_kernel(
         turn_rows(dv_op[0][3], dv_raw[0][1][:, 1, :], "scalar")
         turn_rows(dv_op[1][0], dv_raw[1][0][:, 0, :], "scalar")
         turn_rows(dv_op[1][1], dv_raw[1][0][:, 1, :], "vector")
-        project(0, "scalar")
         turn_rows(dv_op[1][2], dv_raw[1][1][:, 0, :], "scalar")
-        turn_rows(dv_op[1][3], dv_raw[1][1][:, 1, :], "vector")
+        turn_rows(dv_op[1][3], dv_raw[1][1][:, 1, :], "scalar")
+        project(0, "scalar")
         turn_pass(w_op[0][0], w1_raw, 0, "scalar")
-        turn_pass(w_op[0][1], w1_raw, 1, "scalar")
+        turn_pass(w_op[0][1], w1_raw, 1, "vector")
         turn_pass(du_op[0], du1_raw, 0, "scalar")
-        project(1, "vector")
         turn_pass(w_op[1][0], w3_raw, 0, "scalar")
         turn_pass(w_op[1][1], w3_raw, 1, "scalar")
         turn_half(du_op[1], du3_raw[0][:], 0, "vector")
+        project(1, "scalar")
         turn_half(du_op[1], du3_raw[1][:], 1, "scalar")
 
         gate = sums.tile([P, I], F32, name="gate")

@@ -41,14 +41,14 @@ def empty(nc, engine, out, in_):
         nc.scalar.copy(out=out, in_=in_)
 
 
-def turn(nc, banks, identity, sources, grouped, order, engine):
+def turn(nc, banks, identity, sources, grouped, engine):
     n = len(sources)
     bank = banks.tile([P, BANK_PLANES, P], F32, name="bank")
     for s, words in enumerate(sources):
         for u in range(2):
             nc.tensor.transpose(bank[:, 2 * s + u, :], words[:, u * P : (u + 1) * P], identity[:])
-    turned = bank[:, : 2 * n, :].rearrange("p (s u) r -> p " + order + " u", u=2)
-    empty(nc, engine, grouped.bitcast(F32).rearrange("p (" + order + " u) -> p " + order + " u", s=n, u=2), turned)
+    turned = bank[:, : 2 * n, :].rearrange("p (s u) r -> p s r u", u=2)
+    empty(nc, engine, grouped.bitcast(F32).rearrange("p (s r u) -> p s r u", s=n, u=2), turned)
 
 
 def quantise(nc, operand, first, n):
@@ -94,9 +94,10 @@ def tile_merge_mixtralsparsemoeblock_pa_s_kernel(
             [load("dv%d_raw%d" % (n, u), [P, 2, H], dv.rearrange("(u m e) k -> u m e k", u=2, e=2)[u]) for u in range(2)]
             for n, dv in enumerate((dv1, dv3))
         ]
-        w1_raw = load("w1_raw", [P, 2, H], Wmean1.rearrange("(m e) k -> m e k", e=2))
-        du1_raw = load("du1_raw", [P, 2, R], du1.rearrange("(m e) k -> m e k", e=2))
-        w3_raw = load("w3_raw", [P, 2, H], Wmean3.rearrange("(m e) k -> m e k", e=2))
+        w1_both = load("w1_raw", [P, 2, H], Wmean1.rearrange("(c m) k -> m c k", c=2))
+        du1_both = load("du1_raw", [P, 2, R], du1.rearrange("(c m) k -> m c k", c=2))
+        w3_raw = [load("w3_raw%d" % c, [P, H], Wmean3[c * P : (c + 1) * P, :]) for c in range(2)]
+        w_rows = [[w1_both[:, c, :] for c in range(2)], [raw[:] for raw in w3_raw]]
         du3_raw = [load("du3_raw%d" % c, [P, R], du3[c * P : (c + 1) * P, :]) for c in range(2)]
 
         identity = keep.tile([P, P], F32, name="identity")
@@ -113,7 +114,7 @@ def tile_merge_mixtralsparsemoeblock_pa_s_kernel(
 
         x_op = new_operand(keep, "x", H_PASSES * P)
         dv_op = [[new_operand(keep, "dv%d_%d" % (n, j), H_PASSES * P) for j in range(PACK)] for n in range(2)]
-        w_op = [[new_operand(keep, "w%d_%d" % (n, g), I) for g in range(H_PASSES)] for n in range(2)]
+        w_op = [[new_operand(keep, "w%d_%d" % (n, c), H_PASSES * P) for c in range(2)] for n in range(2)]
         du_op = [new_operand(keep, "du%d" % n, I) for n in range(2)]
         p_op = [new_operand(keep, "p%d" % n, T) for n in range(2)]
         p_bank = [sums.tile([P, PACK, T], F32, name="p%d_bank" % n, tag="side%d" % n) for n in range(2)]
@@ -127,16 +128,16 @@ def tile_merge_mixtralsparsemoeblock_pa_s_kernel(
             copied.extend(todo)
 
         def turn_rows(operand, row, engine):
-            turn(nc, banks, identity, [pairs(row, g) for g in range(H_PASSES)], operand["grouped"][:], "s r", engine)
+            turn(nc, banks, identity, [pairs(row, g) for g in range(H_PASSES)], operand["grouped"][:], engine)
             step([(operand, 0, H_PASSES)])
 
-        def turn_pass(operand, raw, g, engine):
-            turn(nc, banks, identity, [pairs(raw[:, e, :], g) for e in range(2)], operand["grouped"][:], "r s", engine)
+        def turn_du(operand, both, engine):
+            turn(nc, banks, identity, [pairs(both[:, c, :], 0) for c in range(2)], operand["grouped"][:], engine)
             step([(operand, 0, 2)])
 
         def turn_half(operand, raw, c, engine):
             cols = slice(c * P * PACK, (c + 1) * P * PACK)
-            turn(nc, banks, identity, [pairs(raw, 0)], operand["grouped"][:, cols], "s r", engine)
+            turn(nc, banks, identity, [pairs(raw, 0)], operand["grouped"][:, cols], engine)
             step([(operand, c, 1)])
 
         def project(n, engine):
@@ -161,26 +162,28 @@ def tile_merge_mixtralsparsemoeblock_pa_s_kernel(
         turn_rows(dv_op[1][2], dv_raw[1][1][:, 0, :], "scalar")
         turn_rows(dv_op[1][3], dv_raw[1][1][:, 1, :], "scalar")
         project(0, "scalar")
-        turn_pass(w_op[0][0], w1_raw, 0, "scalar")
-        turn_pass(w_op[0][1], w1_raw, 1, "vector")
-        turn_pass(du_op[0], du1_raw, 0, "scalar")
-        turn_pass(w_op[1][0], w3_raw, 0, "scalar")
-        turn_pass(w_op[1][1], w3_raw, 1, "scalar")
+        turn_rows(w_op[0][0], w_rows[0][0], "scalar")
+        turn_rows(w_op[0][1], w_rows[0][1], "vector")
+        turn_du(du_op[0], du1_both, "scalar")
+        turn_rows(w_op[1][0], w_rows[1][0], "scalar")
+        turn_rows(w_op[1][1], w_rows[1][1], "scalar")
         turn_half(du_op[1], du3_raw[0][:], 0, "vector")
         project(1, "scalar")
         turn_half(du_op[1], du3_raw[1][:], 1, "scalar")
 
         gate = sums.tile([P, I], F32, name="gate")
-        for g in range(H_PASSES):
-            mx_pass(nc, gate[:], x_op, g, w_op[0][g], 0, 2, start=(g == 0), stop=False)
-        mx_pass(nc, gate[:], p_op[0], 0, du_op[0], 0, 2, start=False, stop=True)
+        for c in range(2):
+            half = gate[:, c * P : (c + 1) * P]
+            for g in range(H_PASSES):
+                mx_pass(nc, half, x_op, g, w_op[0][c], g, 1, start=(g == 0), stop=False)
+            mx_pass(nc, half, p_op[0], 0, du_op[0], c, 1, start=False, stop=True)
         silu_gate = keep.tile([P, I], F32, name="silu_gate")
         nc.scalar.activation(out=silu_gate[:], in_=gate[:], func=SILU)
         step([])
         up = [sums.tile([P, P], F32, name="up%d" % c, tag="side%d" % c) for c in range(2)]
         for c in range(2):
             for g in range(H_PASSES):
-                mx_pass(nc, up[c][:], x_op, g, w_op[1][g], c, 1, start=(g == 0), stop=False)
+                mx_pass(nc, up[c][:], x_op, g, w_op[1][c], g, 1, start=(g == 0), stop=False)
         z = keep.tile([P, I], F32, name="z")
         for c in range(2):
             cols = slice(c * P, (c + 1) * P)

@@ -90,14 +90,19 @@ def tile_merge_mixtralsparsemoeblock_pa_s_kernel(
             return raw
 
         x_raw = load("x_raw", [P, H], x)
-        dv_raw = [
-            [load("dv%d_raw%d" % (n, u), [P, 2, H], dv.rearrange("(u m e) k -> u m e k", u=2, e=2)[u]) for u in range(2)]
-            for n, dv in enumerate((dv1, dv3))
-        ]
-        w1_both = load("w1_raw", [P, 2, H], Wmean1.rearrange("(c m) k -> m c k", c=2))
+        def load_dv(n, dv):
+            rows = dv.rearrange("(u m e) k -> u m e k", u=2, e=2)
+            return [load("dv%d_raw%d" % (n, u), [P, 2, H], rows[u]) for u in range(2)]
+
+        def load_w(n, w):
+            raw = [load("w%d_raw%d" % (n, c), [P, H], w[c * P : (c + 1) * P, :]) for c in range(2)]
+            return [half[:] for half in raw]
+
+        dv_raw = [load_dv(0, dv1)]
+        w_rows = [load_w(0, Wmean1)]
+        dv_raw.append(load_dv(1, dv3))
         du1_both = load("du1_raw", [P, 2, R], du1.rearrange("(c m) k -> m c k", c=2))
-        w3_raw = [load("w3_raw%d" % c, [P, H], Wmean3[c * P : (c + 1) * P, :]) for c in range(2)]
-        w_rows = [[w1_both[:, c, :] for c in range(2)], [raw[:] for raw in w3_raw]]
+        w_rows.append(load_w(1, Wmean3))
         du3_raw = [load("du3_raw%d" % c, [P, R], du3[c * P : (c + 1) * P, :]) for c in range(2)]
 
         identity = keep.tile([P, P], F32, name="identity")
@@ -154,20 +159,20 @@ def tile_merge_mixtralsparsemoeblock_pa_s_kernel(
 
         turn_rows(x_op, x_raw[:], "scalar")
         turn_rows(dv_op[0][0], dv_raw[0][0][:, 0, :], "scalar")
-        turn_rows(dv_op[0][1], dv_raw[0][0][:, 1, :], "vector")
-        turn_rows(dv_op[0][2], dv_raw[0][1][:, 0, :], "scalar")
+        turn_rows(dv_op[0][1], dv_raw[0][0][:, 1, :], "scalar")
+        turn_rows(dv_op[0][2], dv_raw[0][1][:, 0, :], "vector")
         turn_rows(dv_op[0][3], dv_raw[0][1][:, 1, :], "scalar")
+        turn_rows(w_op[0][0], w_rows[0][0], "scalar")
+        turn_rows(w_op[0][1], w_rows[0][1], "scalar")
+        project(0, "scalar")
         turn_rows(dv_op[1][0], dv_raw[1][0][:, 0, :], "scalar")
         turn_rows(dv_op[1][1], dv_raw[1][0][:, 1, :], "vector")
         turn_rows(dv_op[1][2], dv_raw[1][1][:, 0, :], "scalar")
         turn_rows(dv_op[1][3], dv_raw[1][1][:, 1, :], "scalar")
-        project(0, "scalar")
-        turn_rows(w_op[0][0], w_rows[0][0], "scalar")
-        turn_rows(w_op[0][1], w_rows[0][1], "vector")
         turn_du(du_op[0], du1_both, "scalar")
-        turn_rows(w_op[1][0], w_rows[1][0], "scalar")
+        turn_rows(w_op[1][0], w_rows[1][0], "vector")
         turn_rows(w_op[1][1], w_rows[1][1], "scalar")
-        turn_half(du_op[1], du3_raw[0][:], 0, "vector")
+        turn_half(du_op[1], du3_raw[0][:], 0, "scalar")
         project(1, "scalar")
         turn_half(du_op[1], du3_raw[1][:], 1, "scalar")
 

@@ -17,7 +17,7 @@ PACK = 4
 K_PASS = P * PACK
 H_PASSES = H // K_PASS
 BANK_PLANES = 4
-WARM_PASSES = 10
+WARM_PASSES = 7
 
 FLOPS = 2 * T * (2 * H * I + 2 * H * R + 2 * R * I)
 
@@ -110,12 +110,12 @@ def tile_merge_mixtralsparsemoeblock_pa_s_kernel(
         warm = keep.tile([P, 1], F32, name="warm")
         nc.vector.memset(warm[:], 0.0)
         nc.scalar.activation(out=warm[:], in_=warm[:], func=SILU)
-        zeros = new_operand(keep, "zeros", P)
+        zeros = new_operand(keep, "zeros", 2 * P)
         nc.vector.memset(zeros["grouped"][:].bitcast(I32), 0)
-        quantise(nc, zeros, 0, 1)
+        quantise(nc, zeros, 0, 2)
         idle = banks.tile([P, BANK_PLANES, P], F32, name="bank")
         for i in range(WARM_PASSES):
-            mx_pass(nc, idle[:, 0, :], zeros, 0, zeros, 0, 1, start=True, stop=True)
+            mx_pass(nc, idle[:, :2, :].rearrange("p a r -> p (a r)"), zeros, 0, zeros, 0, 2, start=True, stop=True)
 
         x_op = new_operand(keep, "x", H_PASSES * P)
         dv_op = [[new_operand(keep, "dv%d_%d" % (n, j), H_PASSES * P) for j in range(PACK)] for n in range(2)]

@@ -5,7 +5,6 @@ from concourse.masks import make_identity
 
 F32 = mybir.dt.float32
 BF16 = mybir.dt.bfloat16
-I32 = mybir.dt.int32
 U32 = mybir.dt.uint32
 U8 = mybir.dt.uint8
 FP8X4 = mybir.dt.float8_e4m3fn_x4
@@ -17,7 +16,7 @@ PACK = 4
 K_PASS = P * PACK
 H_PASSES = H // K_PASS
 BANK_PLANES = 4
-WARM_PASSES = 7
+WARM_MATMULS = 4
 
 FLOPS = 2 * T * (2 * H * I + 2 * H * R + 2 * R * I)
 
@@ -107,15 +106,14 @@ def tile_merge_mixtralsparsemoeblock_pa_s_kernel(
 
         identity = keep.tile([P, P], F32, name="identity")
         make_identity(nc, identity[:])
+        zeros = keep.tile([P, P], F32, name="zeros")
+        nc.vector.memset(zeros[:], 0.0)
+        idle = banks.tile([P, BANK_PLANES, P], F32, name="bank")
+        for i in range(WARM_MATMULS):
+            nc.tensor.matmul(idle[:, 0, :], lhsT=zeros[:], rhs=zeros[:], start=True, stop=True)
         warm = keep.tile([P, 1], F32, name="warm")
         nc.vector.memset(warm[:], 0.0)
         nc.scalar.activation(out=warm[:], in_=warm[:], func=SILU)
-        zeros = new_operand(keep, "zeros", 2 * P)
-        nc.vector.memset(zeros["grouped"][:].bitcast(I32), 0)
-        quantise(nc, zeros, 0, 2)
-        idle = banks.tile([P, BANK_PLANES, P], F32, name="bank")
-        for i in range(WARM_PASSES):
-            mx_pass(nc, idle[:, :2, :].rearrange("p a r -> p (a r)"), zeros, 0, zeros, 0, 2, start=True, stop=True)
 
         x_op = new_operand(keep, "x", H_PASSES * P)
         dv_op = [[new_operand(keep, "dv%d_%d" % (n, j), H_PASSES * P) for j in range(PACK)] for n in range(2)]

@@ -16,6 +16,7 @@ PACK = 4
 K_PASS = P * PACK
 H_PASSES = H // K_PASS
 BANK_PLANES = 4
+KEEP_COLS = 128
 WARM_MATMULS = 4
 
 FLOPS = 2 * T * (2 * H * I + 2 * H * R + 2 * R * I)
@@ -130,6 +131,11 @@ def tile_merge_mixtralsparsemoeblock_pa_s_kernel(
             copied.clear()
             copied.extend(todo)
 
+        gate = sums.tile([P, I], F32, name="gate")
+
+        def keep_clock():
+            nc.tensor.matmul(gate[:, :KEEP_COLS], lhsT=identity[:], rhs=identity[:, :KEEP_COLS], start=True, stop=True)
+
         def turn_rows(operand, row, engine):
             turn(nc, banks, identity, [pairs(row, g) for g in range(H_PASSES)], operand["grouped"][:], engine)
             step([(operand, 0, H_PASSES)])
@@ -156,25 +162,31 @@ def tile_merge_mixtralsparsemoeblock_pa_s_kernel(
             copied.append((p_op[n], 0, 1))
 
         turn_rows(x_op, x_raw[:], "scalar")
+        keep_clock()
         turn_rows(dv_op[0][0], dv_raw[0][0][:, 0, :], "scalar")
         turn_rows(dv_op[0][1], dv_raw[0][0][:, 1, :], "scalar")
+        keep_clock()
         turn_rows(dv_op[0][2], dv_raw[0][1][:, 0, :], "vector")
         turn_rows(dv_op[0][3], dv_raw[0][1][:, 1, :], "scalar")
+        keep_clock()
         turn_rows(w_op[0][0], w_rows[0][0], "scalar")
         turn_rows(w_op[0][1], w_rows[0][1], "scalar")
         project(0, "scalar")
+        keep_clock()
         turn_rows(dv_op[1][0], dv_raw[1][0][:, 0, :], "scalar")
         turn_rows(dv_op[1][1], dv_raw[1][0][:, 1, :], "vector")
+        keep_clock()
         turn_rows(dv_op[1][2], dv_raw[1][1][:, 0, :], "scalar")
         turn_rows(dv_op[1][3], dv_raw[1][1][:, 1, :], "scalar")
+        keep_clock()
         turn_du(du_op[0], du1_both, "scalar")
+        keep_clock()
         turn_rows(w_op[1][0], w_rows[1][0], "vector")
         turn_rows(w_op[1][1], w_rows[1][1], "scalar")
         turn_half(du_op[1], du3_raw[0][:], 0, "scalar")
         project(1, "scalar")
         turn_half(du_op[1], du3_raw[1][:], 1, "scalar")
 
-        gate = sums.tile([P, I], F32, name="gate")
         for c in range(2):
             half = gate[:, c * P : (c + 1) * P]
             for g in range(H_PASSES):

@@ -51,6 +51,15 @@ def turn(nc, banks, identity, sources, grouped, engine):
     empty(nc, engine, grouped.bitcast(F32).rearrange("p (s r u) -> p s r u", s=n, u=2), turned)
 
 
+def turn_pairs(nc, banks, identity, slots, grouped, engine):
+    bank = banks.tile([P, BANK_PLANES, P], F32, name="bank")
+    for c, words in enumerate(slots):
+        for u in range(2):
+            nc.tensor.transpose(bank[:, 2 * c + u, :], words[:, u * P : (u + 1) * P], identity[:])
+    turned = bank[:].rearrange("p (c u) m -> p m c u", u=2)
+    empty(nc, engine, grouped.bitcast(F32).rearrange("p (m c u) -> p m c u", c=2, u=2), turned)
+
+
 def quantise(nc, operand, first, n):
     cols = slice(first * P, (first + n) * P)
     nc.vector.quantize_mx(
@@ -94,15 +103,14 @@ def tile_merge_mixtralsparsemoeblock_pa_s_kernel(
             rows = dv.rearrange("(u m e) k -> u m e k", u=2, e=2)
             return [load("dv%d_raw%d" % (n, u), [P, 2, H], rows[u]) for u in range(2)]
 
-        def load_w(n, w):
-            raw = [load("w%d_raw%d" % (n, c), [P, H], w[c * P : (c + 1) * P, :]) for c in range(2)]
-            return [half[:] for half in raw]
+        def load_pairs(name, w):
+            return load(name, [P, 2, w.shape[1]], w.rearrange("(m c) k -> m c k", c=2))
 
         dv_raw = [load_dv(0, dv1)]
-        w_rows = [load_w(0, Wmean1)]
+        w_raw = [load_pairs("w0_raw", Wmean1)]
         dv_raw.append(load_dv(1, dv3))
-        du1_both = load("du1_raw", [P, 2, R], du1.rearrange("(c m) k -> m c k", c=2))
-        w_rows.append(load_w(1, Wmean3))
+        du1_raw = load_pairs("du1_raw", du1)
+        w_raw.append(load_pairs("w1_raw", Wmean3))
         du3_raw = [load("du3_raw%d" % c, [P, R], du3[c * P : (c + 1) * P, :]) for c in range(2)]
 
         identity = keep.tile([P, P], F32, name="identity")
@@ -118,7 +126,7 @@ def tile_merge_mixtralsparsemoeblock_pa_s_kernel(
 
         x_op = new_operand(keep, "x", H_PASSES * P)
         dv_op = [[new_operand(keep, "dv%d_%d" % (n, j), H_PASSES * P) for j in range(PACK)] for n in range(2)]
-        w_op = [[new_operand(keep, "w%d_%d" % (n, c), H_PASSES * P) for c in range(2)] for n in range(2)]
+        w_op = [new_operand(keep, "w%d" % n, H_PASSES * I) for n in range(2)]
         du_op = [new_operand(keep, "du%d" % n, I) for n in range(2)]
         p_op = [new_operand(keep, "p%d" % n, T) for n in range(2)]
         p_bank = [sums.tile([P, PACK, T], F32, name="p%d_bank" % n, tag="side%d" % n) for n in range(2)]
@@ -140,9 +148,10 @@ def tile_merge_mixtralsparsemoeblock_pa_s_kernel(
             turn(nc, banks, identity, [pairs(row, g) for g in range(H_PASSES)], operand["grouped"][:], engine)
             step([(operand, 0, H_PASSES)])
 
-        def turn_du(operand, both, engine):
-            turn(nc, banks, identity, [pairs(both[:, c, :], 0) for c in range(2)], operand["grouped"][:], engine)
-            step([(operand, 0, 2)])
+        def turn_pass(operand, raw, g, engine):
+            cols = slice(g * I * PACK, (g + 1) * I * PACK)
+            turn_pairs(nc, banks, identity, [pairs(raw[:, c, :], g) for c in range(2)], operand["grouped"][:, cols], engine)
+            step([(operand, 2 * g, 2)])
 
         def turn_half(operand, raw, c, engine):
             cols = slice(c * P * PACK, (c + 1) * P * PACK)
@@ -169,8 +178,8 @@ def tile_merge_mixtralsparsemoeblock_pa_s_kernel(
         turn_rows(dv_op[0][2], dv_raw[0][1][:, 0, :], "vector")
         turn_rows(dv_op[0][3], dv_raw[0][1][:, 1, :], "scalar")
         keep_clock()
-        turn_rows(w_op[0][0], w_rows[0][0], "scalar")
-        turn_rows(w_op[0][1], w_rows[0][1], "scalar")
+        turn_pass(w_op[0], w_raw[0], 0, "scalar")
+        turn_pass(w_op[0], w_raw[0], 1, "scalar")
         project(0, "scalar")
         keep_clock()
         turn_rows(dv_op[1][0], dv_raw[1][0][:, 0, :], "scalar")
@@ -179,26 +188,24 @@ def tile_merge_mixtralsparsemoeblock_pa_s_kernel(
         turn_rows(dv_op[1][2], dv_raw[1][1][:, 0, :], "scalar")
         turn_rows(dv_op[1][3], dv_raw[1][1][:, 1, :], "scalar")
         keep_clock()
-        turn_du(du_op[0], du1_both, "scalar")
+        turn_pass(du_op[0], du1_raw, 0, "scalar")
         keep_clock()
-        turn_rows(w_op[1][0], w_rows[1][0], "vector")
-        turn_rows(w_op[1][1], w_rows[1][1], "scalar")
+        turn_pass(w_op[1], w_raw[1], 0, "vector")
+        turn_pass(w_op[1], w_raw[1], 1, "scalar")
         turn_half(du_op[1], du3_raw[0][:], 0, "scalar")
         project(1, "scalar")
         turn_half(du_op[1], du3_raw[1][:], 1, "scalar")
 
-        for c in range(2):
-            half = gate[:, c * P : (c + 1) * P]
-            for g in range(H_PASSES):
-                mx_pass(nc, half, x_op, g, w_op[0][c], g, 1, start=(g == 0), stop=False)
-            mx_pass(nc, half, p_op[0], 0, du_op[0], c, 1, start=False, stop=True)
+        for g in range(H_PASSES):
+            mx_pass(nc, gate[:], x_op, g, w_op[0], 2 * g, 2, start=(g == 0), stop=False)
+        mx_pass(nc, gate[:], p_op[0], 0, du_op[0], 0, 2, start=False, stop=True)
         silu_gate = keep.tile([P, I], F32, name="silu_gate")
         nc.scalar.activation(out=silu_gate[:], in_=gate[:], func=SILU)
         step([])
         up = [sums.tile([P, P], F32, name="up%d" % c, tag="side%d" % c) for c in range(2)]
         for c in range(2):
             for g in range(H_PASSES):
-                mx_pass(nc, up[c][:], x_op, g, w_op[1][c], g, 1, start=(g == 0), stop=False)
+                mx_pass(nc, up[c][:], x_op, g, w_op[1], 2 * g + c, 1, start=(g == 0), stop=False)
         z = keep.tile([P, I], F32, name="z")
         for c in range(2):
             cols = slice(c * P, (c + 1) * P)

from contextlib import ExitStack

import concourse.mybir as mybir
from concourse.masks import make_identity

F32 = mybir.dt.float32
BF16 = mybir.dt.bfloat16
U32 = mybir.dt.uint32
U8 = mybir.dt.uint8
FP8X4 = mybir.dt.float8_e4m3fn_x4
SILU = mybir.ActivationFunctionType.Silu

P = 128
T, H, I, R = 128, 1024, 256, 512
PACK = 4
K_PASS = P * PACK
H_PASSES = H // K_PASS
BANK_PLANES = 4
KEEP_COLS = 128
WARM_MATMULS = 4

FLOPS = 2 * T * (2 * H * I + 2 * H * R + 2 * R * I)


def new_operand(pool, name, cols):
    return {
        "grouped": pool.tile([P, cols * PACK], BF16, name=name + "_grouped", align_bytes=64),
        "codes": pool.tile([P, cols], U32, name=name + "_codes", align_bytes=64),
        "scales": pool.tile([P, cols], U8, name=name + "_scales", align_bytes=64),
    }


def pairs(row, g):
    return row[:, g * K_PASS : (g + 1) * K_PASS].bitcast(F32)


def empty(nc, engine, out, in_):
    if engine == "vector":
        nc.vector.tensor_copy(out=out, in_=in_)
    else:
        nc.scalar.copy(out=out, in_=in_)


def turn(nc, banks, identity, sources, grouped, engine):
    n = len(sources)
    bank = banks.tile([P, BANK_PLANES, P], F32, name="bank")
    for s, words in enumerate(sources):
        for u in range(2):
            nc.tensor.transpose(bank[:, 2 * s + u, :], words[:, u * P : (u + 1) * P], identity[:])
    turned = bank[:, : 2 * n, :].rearrange("p (s u) r -> p s r u", u=2)
    empty(nc, engine, grouped.bitcast(F32).rearrange("p (s r u) -> p s r u", s=n, u=2), turned)


def turn_pairs(nc, banks, identity, slots, grouped, engine):
    bank = banks.tile([P, BANK_PLANES, P], F32, name="bank")
    for c, words in enumerate(slots):
        for u in range(2):
            nc.tensor.transpose(bank[:, 2 * c + u, :], words[:, u * P : (u + 1) * P], identity[:])
    turned = bank[:].rearrange("p (c u) m -> p m c u", u=2)
    empty(nc, engine, grouped.bitcast(F32).rearrange("p (m c u) -> p m c u", c=2, u=2), turned)


def quantise(nc, operand, first, n):
    cols = slice(first * P, (first + n) * P)
    nc.vector.quantize_mx(
        out=operand["codes"][:, cols].bitcast(FP8X4),
        scales=operand["scales"][:, cols],
        in_=operand["grouped"][:, first * P * PACK : (first + n) * P * PACK],
    )


def mx_pass(nc, acc, stationary, s_first, moving, m_first, m_n, start, stop):
    s_cols = slice(s_first * P, (s_first + 1) * P)
    m_cols = slice(m_first * P, (m_first + m_n) * P)
    nc.tensor.matmul_mx(
        out=acc,
        lhsT=stationary["codes"][:, s_cols].bitcast(FP8X4),
        lhsT_scale=stationary["scales"][:, s_cols],
        rhs=moving["codes"][:, m_cols].bitcast(FP8X4),
        rhs_scale=moving["scales"][:, m_cols],
        start=start,
        stop=stop,
    )


def tile_merge_mixtralsparsemoeblock_pa_s_kernel(
    tc, x, Wmean1, Wmean3, du1, dv1, du3, dv3, out
):
    nc = tc.nc
    with ExitStack() as ctx:
        keep = ctx.enter_context(tc.tile_pool(name="keep", bufs=1))
        banks = ctx.enter_context(tc.psum_pool(name="banks", bufs=5))
        sums = ctx.enter_context(tc.psum_pool(name="sums", bufs=1))
        ctx.enter_context(tc.manual_schedule())

        def load(name, shape, rows):
            raw = keep.tile(shape, BF16, name=name)
            nc.sync.dma_start(out=raw[:], in_=rows)
            return raw

        x_raw = load("x_raw", [P, H], x)
        def load_dv(n, dv):
            rows = dv.rearrange("(u m e) k -> u m e k", u=2, e=2)
            return [load("dv%d_raw%d" % (n, u), [P, 2, H], rows[u]) for u in range(2)]

        def load_pairs(name, w):
            return load(name, [P, 2, w.shape[1]], w.rearrange("(m c) k -> m c k", c=2))

        dv_raw = [load_dv(0, dv1)]
        w_raw = [load_pairs("w0_raw", Wmean1)]
        dv_raw.append(load_dv(1, dv3))
        du1_raw = load_pairs("du1_raw", du1)
        w_raw.append(load_pairs("w1_raw", Wmean3))
        du3_raw = [load("du3_raw%d" % c, [P, R], du3[c * P : (c + 1) * P, :]) for c in range(2)]

        identity = keep.tile([P, P], F32, name="identity")
        make_identity(nc, identity[:])
        zeros = keep.tile([P, P], F32, name="zeros")
        nc.vector.memset(zeros[:], 0.0)
        idle = banks.tile([P, BANK_PLANES, P], F32, name="bank")
        for i in range(WARM_MATMULS):
            nc.tensor.matmul(idle[:, 0, :], lhsT=zeros[:], rhs=zeros[:], start=True, stop=True)
        warm = keep.tile([P, 1], F32, name="warm")
        nc.vector.memset(warm[:], 0.0)
        nc.scalar.activation(out=warm[:], in_=warm[:], func=SILU)

        x_op = new_operand(keep, "x", H_PASSES * P)
        dv_op = [[new_operand(keep, "dv%d_%d" % (n, j), H_PASSES * P) for j in range(PACK)] for n in range(2)]
        w_op = [new_operand(keep, "w%d" % n, H_PASSES * I) for n in range(2)]
        du_op = [new_operand(keep, "du%d" % n, I) for n in range(2)]
        p_op = [new_operand(keep, "p%d" % n, T) for n in range(2)]
        p_bank = [sums.tile([P, PACK, T], F32, name="p%d_bank" % n, tag="side%d" % n) for n in range(2)]

        copied = []

        def step(todo):
            for args in copied:
                quantise(nc, *args)
            copied.clear()
            copied.extend(todo)

        gate = sums.tile([P, I], F32, name="gate")

        def keep_clock():
            nc.tensor.matmul(gate[:, :KEEP_COLS], lhsT=identity[:], rhs=identity[:, :KEEP_COLS], start=True, stop=True)

        def turn_rows(operand, row, engine):
            turn(nc, banks, identity, [pairs(row, g) for g in range(H_PASSES)], operand["grouped"][:], engine)
            step([(operand, 0, H_PASSES)])

        def turn_pass(operand, raw, g, engine):
            cols = slice(g * I * PACK, (g + 1) * I * PACK)
            turn_pairs(nc, banks, identity, [pairs(raw[:, c, :], g) for c in range(2)], operand["grouped"][:, cols], engine)
            step([(operand, 2 * g, 2)])

        def turn_half(operand, raw, c, engine):
            cols = slice(c * P * PACK, (c + 1) * P * PACK)
            turn(nc, banks, identity, [pairs(raw, 0)], operand["grouped"][:, cols], engine)
            step([(operand, c, 1)])

        def project(n, engine):
            for j in range(PACK):
                for g in range(H_PASSES):
                    mx_pass(nc, p_bank[n][:, j, :], dv_op[n][j], g, x_op, g, 1, start=(g == 0), stop=(g == H_PASSES - 1))
            empty(
                nc,
                engine,
                p_op[n]["grouped"][:].rearrange("p (t j) -> p t j", j=PACK),
                p_bank[n][:].rearrange("p j t -> p t j"),
            )
            copied.append((p_op[n], 0, 1))

        turn_rows(x_op, x_raw[:], "scalar")
        keep_clock()
        turn_rows(dv_op[0][0], dv_raw[0][0][:, 0, :], "scalar")
        turn_rows(dv_op[0][1], dv_raw[0][0][:, 1, :], "scalar")
        keep_clock()
        turn_rows(dv_op[0][2], dv_raw[0][1][:, 0, :], "vector")
        turn_rows(dv_op[0][3], dv_raw[0][1][:, 1, :], "scalar")
        keep_clock()
        turn_pass(w_op[0], w_raw[0], 0, "scalar")
        turn_pass(w_op[0], w_raw[0], 1, "scalar")
        project(0, "scalar")
        keep_clock()
        turn_rows(dv_op[1][0], dv_raw[1][0][:, 0, :], "scalar")
        turn_rows(dv_op[1][1], dv_raw[1][0][:, 1, :], "vector")
        keep_clock()
        turn_rows(dv_op[1][2], dv_raw[1][1][:, 0, :], "scalar")
        turn_rows(dv_op[1][3], dv_raw[1][1][:, 1, :], "scalar")
        keep_clock()
        turn_pass(du_op[0], du1_raw, 0, "scalar")
        keep_clock()
        turn_pass(w_op[1], w_raw[1], 0, "vector")
        turn_pass(w_op[1], w_raw[1], 1, "scalar")
        turn_half(du_op[1], du3_raw[0][:], 0, "scalar")
        project(1, "scalar")
        turn_half(du_op[1], du3_raw[1][:], 1, "scalar")

        for g in range(H_PASSES):
            mx_pass(nc, gate[:], x_op, g, w_op[0], 2 * g, 2, start=(g == 0), stop=False)
        mx_pass(nc, gate[:], p_op[0], 0, du_op[0], 0, 2, start=False, stop=True)
        silu_gate = keep.tile([P, I], F32, name="silu_gate")
        nc.scalar.activation(out=silu_gate[:], in_=gate[:], func=SILU)
        step([])
        up = [sums.tile([P, P], F32, name="up%d" % c, tag="side%d" % c) for c in range(2)]
        for c in range(2):
            for g in range(H_PASSES):
                mx_pass(nc, up[c][:], x_op, g, w_op[1], 2 * g + c, 1, start=(g == 0), stop=False)
        z = keep.tile([P, I], F32, name="z")
        for c in range(2):
            cols = slice(c * P, (c + 1) * P)
            mx_pass(nc, up[c][:], p_op[1], 0, du_op[1], c, 1, start=False, stop=True)
            nc.vector.tensor_mul(out=z[:, cols], in0=silu_gate[:, cols], in1=up[c][:])
            nc.sync.dma_start(out=out[:, cols], in_=z[:, cols])
